import numpy as np
import ml_dtypes


def mxq(x, axis, fmt="e4m3"):
    dtype, down = {"e4m3": (ml_dtypes.float8_e4m3fn, 7), "e5m2": (ml_dtypes.float8_e5m2, 14)}[fmt]
    v = np.moveaxis(np.asarray(x, np.float32).astype(ml_dtypes.bfloat16).astype(np.float64), axis, -1)
    blocks = v.reshape(v.shape[:-1] + (-1, 32))
    amax = np.abs(blocks).max(-1, keepdims=True)
    byte = np.maximum(np.where(amax > 0, np.frexp(amax)[1] - 1 + 127, 0) - down, 1)
    scale = np.exp2(byte - 127.0)
    codes = (blocks / scale).astype(np.float32).astype(dtype).astype(np.float64)
    return np.moveaxis((codes * scale).reshape(v.shape), -1, axis)


WIDE = False


def mx_kscale(k):
    if not WIDE:
        return np.ones(k)
    levels = np.array([10, -10, 5, -5, 0])
    a = np.random.permutation(np.resize(levels, k // 512 * 4)).reshape(k // 512, 4)
    idx = np.arange(k)
    return np.exp2(a[idx // 512, idx % 128 // 32])


BF16 = ml_dtypes.bfloat16


def bf(x):
    return np.asarray(x, np.float32).astype(BF16)


def f64(x):
    return np.asarray(x).astype(np.float64)


B, D, ELL = 1024, 1024, 4


def setup_inputs():
    s, t = mx_kscale(D), mx_kscale(D)
    return {"x": bf(np.random.standard_normal((B, D))),
            "phi_j": bf(np.random.standard_normal((B, D)) * 0.7 * t / s),
            "phi_k": bf(np.random.standard_normal((B, D)) * 0.7 * s),
            "w_i": bf(np.random.standard_normal((D, D)) / np.sqrt(D) / t),
            "w_j": bf(np.random.standard_normal((D, D)) / np.sqrt(D) * t[:, None] / s)}


def reference(x, phi_j, phi_k, w_i, w_j):
    x, phi_j, phi_k = f64(x), f64(phi_j), f64(phi_k)
    th = np.tanh(x)
    d1 = 1.0 - th * th
    d2 = -2.0 * th * d1
    jvp_jk = mxq(d1 * phi_k, 1, "e4m3") @ mxq(f64(w_j), 1, "e4m3").T
    u = d2 * phi_k * phi_j + d1 * jvp_jk
    return mxq(u, 1, "e4m3") @ mxq(f64(w_i), 1, "e4m3").T

@@ -1,0 +1,218 @@
+from contextlib import ExitStack
+
+import concourse.mybir as mybir
+from concourse.masks import make_identity
+
+FLOPS = 2 * 2 * 1024 * 1024 * 1024
+
+F32 = mybir.dt.float32
+BF16 = mybir.dt.bfloat16
+U32 = mybir.dt.uint32
+U8 = mybir.dt.uint8
+FP8X4 = mybir.dt.float8_e4m3fn_x4
+ACT = mybir.ActivationFunctionType
+ALU = mybir.AluOpType
+
+P = 128
+PACK = 4
+K_PASS = P * PACK
+ROWS = 1024
+D = 1024
+PASSES = D // K_PASS
+ROW_TILES = ROWS // P
+SLOTS = D // P
+HALVES = 2
+PAIR = 2
+BANK = 512
+N_OUT = 512
+SLOTS_PER_QUANTISE = 4
+
+
+def transpose_rows(nc, bank, rows, ident):
+    words = rows.bitcast(F32)
+    for g in range(PASSES):
+        for h in range(HALVES):
+            src = (g * HALVES + h) * P
+            dst = (h * PASSES + g) * P
+            nc.tensor.transpose(bank[:, dst : dst + P], words[:, src : src + P], ident[:])
+
+
+def packed_order(flat):
+    return flat.rearrange("p (c h e) -> p c h e", h=HALVES, e=PAIR)
+
+
+def bank_in_packed_order(bank):
+    return bank[:].bitcast(BF16).rearrange("p (h c e) -> p c h e", h=HALVES, e=PAIR)
+
+
+def tile_inimnetdisc_pa_kernel(tc, x, phi_j, phi_k, w_i, w_j, out):
+    nc = tc.nc
+    with ExitStack() as ctx:
+        const = ctx.enter_context(tc.tile_pool(name="const", bufs=1))
+        inputs = ctx.enter_context(tc.tile_pool(name="inputs", bufs=1))
+        weights = ctx.enter_context(tc.tile_pool(name="weights", bufs=1))
+        wstage = ctx.enter_context(tc.tile_pool(name="wstage", bufs=2))
+        work = ctx.enter_context(tc.tile_pool(name="work", bufs=2))
+        keep = ctx.enter_context(tc.tile_pool(name="keep", bufs=3))
+        mx = ctx.enter_context(tc.tile_pool(name="mx", bufs=3))
+        results = ctx.enter_context(tc.tile_pool(name="results", bufs=3))
+        psum_t = ctx.enter_context(tc.psum_pool(name="psum_t", bufs=4))
+        psum_v = ctx.enter_context(tc.psum_pool(name="psum_v", bufs=2))
+        psum_o = ctx.enter_context(tc.psum_pool(name="psum_o", bufs=2))
+
+        x_rows = x.rearrange("(i p) d -> i p d", p=P)
+        pj_rows = phi_j.rearrange("(i p) d -> i p d", p=P)
+        pk_rows = phi_k.rearrange("(i p) d -> i p d", p=P)
+        out_rows = out.rearrange("(i p) n -> i p n", p=P)
+        wj_view = w_j.rearrange("(c p e) d -> p c e d", p=P, e=PAIR)
+        wi_view = w_i.rearrange("(c e p) d -> p c e d", p=P, e=PAIR)
+
+        x_sb, pj_sb, pk_sb = [], [], []
+
+        def load_row_tile(i):
+            x_sb.append(inputs.tile([P, D], BF16, name="x%d" % i))
+            pj_sb.append(inputs.tile([P, D], BF16, name="pj%d" % i))
+            pk_sb.append(inputs.tile([P, D], BF16, name="pk%d" % i))
+            nc.sync.dma_start(out=x_sb[i][:], in_=x_rows[i])
+            nc.sync.dma_start(out=pj_sb[i][:], in_=pj_rows[i])
+            nc.sync.dma_start(out=pk_sb[i][:], in_=pk_rows[i])
+
+        def load_weight(view, name):
+            raw = []
+            for c in range(SLOTS // PAIR):
+                raw.append(weights.tile([P, PAIR, D], BF16, name="%s_raw%d" % (name, c)))
+                nc.sync.dma_start(out=raw[c][:], in_=view[:, c])
+            return raw
+
+        load_row_tile(0)
+        wj_raw = load_weight(wj_view, "wj")
+        load_row_tile(1)
+        wi_raw = load_weight(wi_view, "wi")
+        for i in range(2, ROW_TILES):
+            load_row_tile(i)
+
+        ident = const.tile([P, P], F32)
+        make_identity(nc, ident[:])
+
+        def quantise_weight(raw, name):
+            codes = weights.tile([P, PASSES, D], U32, name="%s_codes" % name, align_bytes=64)
+            scales = weights.tile([P, PASSES, D], U8, name="%s_scales" % name, align_bytes=64)
+            width = SLOTS_PER_QUANTISE * P
+            for first in range(0, SLOTS, SLOTS_PER_QUANTISE):
+                grouped = wstage.tile([P, PASSES * width * PACK], BF16, align_bytes=64)
+                grouped_words = grouped[:].bitcast(F32).rearrange(
+                    "p (g s c h) -> p g s c h", g=PASSES, s=SLOTS_PER_QUANTISE, h=HALVES
+                )
+                for s in range(SLOTS_PER_QUANTISE):
+                    slot = first + s
+                    w_bank = psum_t.tile([P, BANK], F32, tag="bank")
+                    transpose_rows(nc, w_bank, raw[slot // PAIR][:, slot % PAIR, :], ident)
+                    nc.scalar.copy(
+                        out=grouped_words[:, :, s, :, :],
+                        in_=w_bank[:].rearrange("p (h g c) -> p g c h", h=HALVES, g=PASSES),
+                    )
+                for g in range(PASSES):
+                    cols = slice(first * P, first * P + width)
+                    nc.vector.quantize_mx(
+                        out=codes[:, g, cols].bitcast(FP8X4),
+                        scales=scales[:, g, cols],
+                        in_=grouped[:, g * width * PACK : (g + 1) * width * PACK],
+                    )
+            return codes, scales
+
+        d1_of, q_of, g_of, u_of = {}, {}, {}, {}
+
+        def stage_a(i):
+            x_bank = psum_t.tile([P, BANK], F32, tag="bank")
+            transpose_rows(nc, x_bank, x_sb[i][:], ident)
+            pj_bank = psum_t.tile([P, BANK], F32, tag="bank")
+            transpose_rows(nc, pj_bank, pj_sb[i][:], ident)
+            pk_bank = psum_t.tile([P, BANK], F32, tag="bank")
+            transpose_rows(nc, pk_bank, pk_sb[i][:], ident)
+
+            th = work.tile([P, D], F32)
+            nc.scalar.activation(out=packed_order(th[:]), in_=bank_in_packed_order(x_bank), func=ACT.Tanh)
+            sq = work.tile([P, D], F32)
+            nc.scalar.activation(out=sq[:], in_=th[:], func=ACT.Square)
+            d1 = keep.tile([P, D], F32)
+            nc.scalar.activation(out=d1[:], in_=sq[:], func=ACT.Copy, scale=-1.0, bias=1.0)
+
+            tj = work.tile([P, D], F32)
+            nc.vector.tensor_tensor(
+                out=packed_order(tj[:]), in0=packed_order(th[:]), in1=bank_in_packed_order(pj_bank), op=ALU.mult
+            )
+            g_bf = mx.tile([P, D], BF16, align_bytes=64)
+            nc.vector.tensor_tensor(
+                out=packed_order(g_bf[:]), in0=packed_order(d1[:]), in1=bank_in_packed_order(pk_bank), op=ALU.mult
+            )
+            q = keep.tile([P, D], F32)
+            nc.vector.tensor_tensor(
+                out=packed_order(q[:]), in0=packed_order(tj[:]), in1=bank_in_packed_order(pk_bank), op=ALU.mult
+            )
+            g_codes = mx.tile([P, PASSES * P], U32, align_bytes=64)
+            g_scales = mx.tile([P, PASSES * P], U8, align_bytes=64)
+            nc.vector.quantize_mx(out=g_codes[:].bitcast(FP8X4), scales=g_scales[:], in_=g_bf[:])
+            d1_of[i], q_of[i], g_of[i] = d1, q, (g_codes, g_scales)
+
+        def stage_b(i):
+            g_codes, g_scales = g_of[i]
+            d1, q = d1_of[i], q_of[i]
+            s_sum = work.tile([P, D], F32)
+            for g2 in range(PASSES):
+                v_bank = psum_v.tile([P, BANK], F32)
+                for t in range(PACK):
+                    slot = g2 * PACK + t
+                    for g in range(PASSES):
+                        nc.tensor.matmul_mx(
+                            out=v_bank[:, t * P : (t + 1) * P],
+                            lhsT=wj_codes[:, g, slot * P : (slot + 1) * P].bitcast(FP8X4),
+                            lhsT_scale=wj_scales[:, g, slot * P : (slot + 1) * P],
+                            rhs=g_codes[:, g * P : (g + 1) * P].bitcast(FP8X4),
+                            rhs_scale=g_scales[:, g * P : (g + 1) * P],
+                            start=(g == 0),
+                            stop=(g == PASSES - 1),
+                        )
+                part = slice(g2 * K_PASS, (g2 + 1) * K_PASS)
+                nc.vector.scalar_tensor_tensor(
+                    out=s_sum[:, part].rearrange("p (r t) -> p r t", t=PACK),
+                    in0=q[:, part].rearrange("p (r t) -> p r t", t=PACK),
+                    scalar=-2.0,
+                    in1=v_bank[:].rearrange("p (t r) -> p r t", t=PACK),
+                    op0=ALU.mult,
+                    op1=ALU.add,
+                )
+            u_bf = mx.tile([P, D], BF16, align_bytes=64)
+            nc.vector.tensor_tensor(out=u_bf[:], in0=s_sum[:], in1=d1[:], op=ALU.mult)
+            u_codes = mx.tile([P, PASSES * P], U32, align_bytes=64)
+            u_scales = mx.tile([P, PASSES * P], U8, align_bytes=64)
+            nc.vector.quantize_mx(out=u_codes[:].bitcast(FP8X4), scales=u_scales[:], in_=u_bf[:])
+            u_of[i] = (u_codes, u_scales)
+
+        def stage_c(i):
+            u_codes, u_scales = u_of[i]
+            out_sb = results.tile([P, D], F32)
+            for n in range(D // N_OUT):
+                cols = slice(n * N_OUT, (n + 1) * N_OUT)
+                o_bank = psum_o.tile([P, BANK], F32)
+                for g2 in range(PASSES):
+                    nc.tensor.matmul_mx(
+                        out=o_bank[:],
+                        lhsT=u_codes[:, g2 * P : (g2 + 1) * P].bitcast(FP8X4),
+                        lhsT_scale=u_scales[:, g2 * P : (g2 + 1) * P],
+                        rhs=wi_codes[:, g2, cols].bitcast(FP8X4),
+                        rhs_scale=wi_scales[:, g2, cols],
+                        start=(g2 == 0),
+                        stop=(g2 == PASSES - 1),
+                    )
+                nc.scalar.copy(out=out_sb[:, cols], in_=o_bank[:])
+            nc.sync.dma_start(out=out_rows[i], in_=out_sb[:])
+
+        stage_a(0)
+        wj_codes, wj_scales = quantise_weight(wj_raw, "wj")
+        stage_a(1)
+        wi_codes, wi_scales = quantise_weight(wi_raw, "wi")
+        for i in range(ROW_TILES):
+            stage_b(i)
+            if i + 2 < ROW_TILES:
+                stage_a(i + 2)
+            stage_c(i)

@@ -135,7 +135,7 @@ def tile_inimnetdisc_pa_kernel(tc, x, phi_j, phi_k, w_i, w_j, out):
             sq = work.tile([P, D], F32)
             nc.scalar.activation(out=sq[:], in_=th[:], func=ACT.Square)
             d1 = keep.tile([P, D], F32)
-            nc.scalar.activation(out=d1[:], in_=sq[:], func=ACT.Copy, scale=-1.0, bias=1.0)
+            nc.gpsimd.tensor_scalar(out=d1[:], in0=sq[:], scalar1=-1.0, scalar2=1.0, op0=ALU.mult, op1=ALU.add)
 
             tj = work.tile([P, D], F32)
             nc.vector.tensor_tensor(
@@ -182,7 +182,7 @@ def tile_inimnetdisc_pa_kernel(tc, x, phi_j, phi_k, w_i, w_j, out):
                     op1=ALU.add,
                 )
             u_bf = mx.tile([P, D], BF16, align_bytes=64)
-            nc.vector.tensor_tensor(out=u_bf[:], in0=s_sum[:], in1=d1[:], op=ALU.mult)
+            nc.gpsimd.tensor_tensor(out=u_bf[:], in0=s_sum[:], in1=d1[:], op=ALU.mult)
             u_codes = mx.tile([P, PASSES * P], U32, align_bytes=64)
             u_scales = mx.tile([P, PASSES * P], U8, align_bytes=64)
             nc.vector.quantize_mx(out=u_codes[:].bitcast(FP8X4), scales=u_scales[:], in_=u_bf[:])
@@ -205,7 +205,7 @@ def tile_inimnetdisc_pa_kernel(tc, x, phi_j, phi_k, w_i, w_j, out):
                         stop=(g2 == PASSES - 1),
                     )
                 nc.scalar.copy(out=out_sb[:, cols], in_=o_bank[:])
-            nc.sync.dma_start(out=out_rows[i], in_=out_sb[:])
+                nc.sync.dma_start(out=out_rows[i][:, cols], in_=out_sb[:, cols])
 
         stage_a(0)
         wj_codes, wj_scales = quantise_weight(wj_raw, "wj")

@@ -26,6 +26,7 @@ PAIR = 2
 BANK = 512
 N_OUT = 512
 SLOTS_PER_QUANTISE = 4
+U_PIECE = 256
 
 
 def transpose_rows(nc, bank, rows, ident):
@@ -135,7 +136,7 @@ def tile_inimnetdisc_pa_kernel(tc, x, phi_j, phi_k, w_i, w_j, out):
             sq = work.tile([P, D], F32)
             nc.scalar.activation(out=sq[:], in_=th[:], func=ACT.Square)
             d1 = keep.tile([P, D], F32)
-            nc.gpsimd.tensor_scalar(out=d1[:], in0=sq[:], scalar1=-1.0, scalar2=1.0, op0=ALU.mult, op1=ALU.add)
+            nc.scalar.activation(out=d1[:], in_=sq[:], func=ACT.Copy, scale=-1.0, bias=1.0)
 
             tj = work.tile([P, D], F32)
             nc.vector.tensor_tensor(
@@ -182,7 +183,9 @@ def tile_inimnetdisc_pa_kernel(tc, x, phi_j, phi_k, w_i, w_j, out):
                     op1=ALU.add,
                 )
             u_bf = mx.tile([P, D], BF16, align_bytes=64)
-            nc.gpsimd.tensor_tensor(out=u_bf[:], in0=s_sum[:], in1=d1[:], op=ALU.mult)
+            for piece in range(0, D, U_PIECE):
+                cut = slice(piece, piece + U_PIECE)
+                nc.gpsimd.tensor_tensor(out=u_bf[:, cut], in0=s_sum[:, cut], in1=d1[:, cut], op=ALU.mult)
             u_codes = mx.tile([P, PASSES * P], U32, align_bytes=64)
             u_scales = mx.tile([P, PASSES * P], U8, align_bytes=64)
             nc.vector.quantize_mx(out=u_codes[:].bitcast(FP8X4), scales=u_scales[:], in_=u_bf[:])

from contextlib import ExitStack

import concourse.mybir as mybir
from concourse.masks import make_identity

FLOPS = 2 * 2 * 1024 * 1024 * 1024

F32 = mybir.dt.float32
BF16 = mybir.dt.bfloat16
U32 = mybir.dt.uint32
U8 = mybir.dt.uint8
FP8X4 = mybir.dt.float8_e4m3fn_x4
ACT = mybir.ActivationFunctionType
ALU = mybir.AluOpType

P = 128
PACK = 4
K_PASS = P * PACK
ROWS = 1024
D = 1024
PASSES = D // K_PASS
ROW_TILES = ROWS // P
SLOTS = D // P
HALVES = 2
PAIR = 2
BANK = 512
N_OUT = 512
SLOTS_PER_QUANTISE = 4
U_PIECE = 256


def transpose_rows(nc, bank, rows, ident):
    words = rows.bitcast(F32)
    for g in range(PASSES):
        for h in range(HALVES):
            src = (g * HALVES + h) * P
            dst = (h * PASSES + g) * P
            nc.tensor.transpose(bank[:, dst : dst + P], words[:, src : src + P], ident[:])


def packed_order(flat):
    return flat.rearrange("p (c h e) -> p c h e", h=HALVES, e=PAIR)


def bank_in_packed_order(bank):
    return bank[:].bitcast(BF16).rearrange("p (h c e) -> p c h e", h=HALVES, e=PAIR)


def tile_inimnetdisc_pa_kernel(tc, x, phi_j, phi_k, w_i, w_j, out):
    nc = tc.nc
    with ExitStack() as ctx:
        const = ctx.enter_context(tc.tile_pool(name="const", bufs=1))
        inputs = ctx.enter_context(tc.tile_pool(name="inputs", bufs=1))
        weights = ctx.enter_context(tc.tile_pool(name="weights", bufs=1))
        wstage = ctx.enter_context(tc.tile_pool(name="wstage", bufs=2))
        work = ctx.enter_context(tc.tile_pool(name="work", bufs=2))
        keep = ctx.enter_context(tc.tile_pool(name="keep", bufs=3))
        mx = ctx.enter_context(tc.tile_pool(name="mx", bufs=3))
        results = ctx.enter_context(tc.tile_pool(name="results", bufs=3))
        psum_t = ctx.enter_context(tc.psum_pool(name="psum_t", bufs=4))
        psum_v = ctx.enter_context(tc.psum_pool(name="psum_v", bufs=2))
        psum_o = ctx.enter_context(tc.psum_pool(name="psum_o", bufs=2))

        x_rows = x.rearrange("(i p) d -> i p d", p=P)
        pj_rows = phi_j.rearrange("(i p) d -> i p d", p=P)
        pk_rows = phi_k.rearrange("(i p) d -> i p d", p=P)
        out_rows = out.rearrange("(i p) n -> i p n", p=P)
        wj_view = w_j.rearrange("(c p e) d -> p c e d", p=P, e=PAIR)
        wi_view = w_i.rearrange("(c e p) d -> p c e d", p=P, e=PAIR)

        x_sb, pj_sb, pk_sb = [], [], []

        def load_row_tile(i):
            x_sb.append(inputs.tile([P, D], BF16, name="x%d" % i))
            pj_sb.append(inputs.tile([P, D], BF16, name="pj%d" % i))
            pk_sb.append(inputs.tile([P, D], BF16, name="pk%d" % i))
            nc.sync.dma_start(out=x_sb[i][:], in_=x_rows[i])
            nc.sync.dma_start(out=pj_sb[i][:], in_=pj_rows[i])
            nc.sync.dma_start(out=pk_sb[i][:], in_=pk_rows[i])

        def load_weight(view, name):
            raw = []
            for c in range(SLOTS // PAIR):
                raw.append(weights.tile([P, PAIR, D], BF16, name="%s_raw%d" % (name, c)))
                nc.sync.dma_start(out=raw[c][:], in_=view[:, c])
            return raw

        load_row_tile(0)
        wj_raw = load_weight(wj_view, "wj")
        load_row_tile(1)
        wi_raw = load_weight(wi_view, "wi")
        for i in range(2, ROW_TILES):
            load_row_tile(i)

        ident = const.tile([P, P], F32)
        make_identity(nc, ident[:])

        def quantise_weight(raw, name):
            codes = weights.tile([P, PASSES, D], U32, name="%s_codes" % name, align_bytes=64)
            scales = weights.tile([P, PASSES, D], U8, name="%s_scales" % name, align_bytes=64)
            width = SLOTS_PER_QUANTISE * P
            for first in range(0, SLOTS, SLOTS_PER_QUANTISE):
                grouped = wstage.tile([P, PASSES * width * PACK], BF16, align_bytes=64)
                grouped_words = grouped[:].bitcast(F32).rearrange(
                    "p (g s c h) -> p g s c h", g=PASSES, s=SLOTS_PER_QUANTISE, h=HALVES
                )
                for s in range(SLOTS_PER_QUANTISE):
                    slot = first + s
                    w_bank = psum_t.tile([P, BANK], F32, tag="bank")
                    transpose_rows(nc, w_bank, raw[slot // PAIR][:, slot % PAIR, :], ident)
                    nc.scalar.copy(
                        out=grouped_words[:, :, s, :, :],
                        in_=w_bank[:].rearrange("p (h g c) -> p g c h", h=HALVES, g=PASSES),
                    )
                for g in range(PASSES):
                    cols = slice(first * P, first * P + width)
                    nc.vector.quantize_mx(
                        out=codes[:, g, cols].bitcast(FP8X4),
                        scales=scales[:, g, cols],
                        in_=grouped[:, g * width * PACK : (g + 1) * width * PACK],
                    )
            return codes, scales

        d1_of, q_of, g_of, u_of = {}, {}, {}, {}

        def stage_a(i):
            x_bank = psum_t.tile([P, BANK], F32, tag="bank")
            transpose_rows(nc, x_bank, x_sb[i][:], ident)
            pj_bank = psum_t.tile([P, BANK], F32, tag="bank")
            transpose_rows(nc, pj_bank, pj_sb[i][:], ident)
            pk_bank = psum_t.tile([P, BANK], F32, tag="bank")
            transpose_rows(nc, pk_bank, pk_sb[i][:], ident)

            th = work.tile([P, D], F32)
            nc.scalar.activation(out=packed_order(th[:]), in_=bank_in_packed_order(x_bank), func=ACT.Tanh)
            sq = work.tile([P, D], F32)
            nc.scalar.activation(out=sq[:], in_=th[:], func=ACT.Square)
            d1 = keep.tile([P, D], F32)
            nc.scalar.activation(out=d1[:], in_=sq[:], func=ACT.Copy, scale=-1.0, bias=1.0)

            tj = work.tile([P, D], F32)
            nc.vector.tensor_tensor(
                out=packed_order(tj[:]), in0=packed_order(th[:]), in1=bank_in_packed_order(pj_bank), op=ALU.mult
            )
            g_bf = mx.tile([P, D], BF16, align_bytes=64)
            nc.vector.tensor_tensor(
                out=packed_order(g_bf[:]), in0=packed_order(d1[:]), in1=bank_in_packed_order(pk_bank), op=ALU.mult
            )
            q = keep.tile([P, D], F32)
            nc.vector.tensor_tensor(
                out=packed_order(q[:]), in0=packed_order(tj[:]), in1=bank_in_packed_order(pk_bank), op=ALU.mult
            )
            g_codes = mx.tile([P, PASSES * P], U32, align_bytes=64)
            g_scales = mx.tile([P, PASSES * P], U8, align_bytes=64)
            nc.vector.quantize_mx(out=g_codes[:].bitcast(FP8X4), scales=g_scales[:], in_=g_bf[:])
            d1_of[i], q_of[i], g_of[i] = d1, q, (g_codes, g_scales)

        def stage_b(i):
            g_codes, g_scales = g_of[i]
            d1, q = d1_of[i], q_of[i]
            s_sum = work.tile([P, D], F32)
            for g2 in range(PASSES):
                v_bank = psum_v.tile([P, BANK], F32)
                for t in range(PACK):
                    slot = g2 * PACK + t
                    for g in range(PASSES):
                        nc.tensor.matmul_mx(
                            out=v_bank[:, t * P : (t + 1) * P],
                            lhsT=wj_codes[:, g, slot * P : (slot + 1) * P].bitcast(FP8X4),
                            lhsT_scale=wj_scales[:, g, slot * P : (slot + 1) * P],
                            rhs=g_codes[:, g * P : (g + 1) * P].bitcast(FP8X4),
                            rhs_scale=g_scales[:, g * P : (g + 1) * P],
                            start=(g == 0),
                            stop=(g == PASSES - 1),
                        )
                part = slice(g2 * K_PASS, (g2 + 1) * K_PASS)
                nc.vector.scalar_tensor_tensor(
                    out=s_sum[:, part].rearrange("p (r t) -> p r t", t=PACK),
                    in0=q[:, part].rearrange("p (r t) -> p r t", t=PACK),
                    scalar=-2.0,
                    in1=v_bank[:].rearrange("p (t r) -> p r t", t=PACK),
                    op0=ALU.mult,
                    op1=ALU.add,
                )
            u_bf = mx.tile([P, D], BF16, align_bytes=64)
            for piece in range(0, D, U_PIECE):
                cut = slice(piece, piece + U_PIECE)
                nc.gpsimd.tensor_tensor(out=u_bf[:, cut], in0=s_sum[:, cut], in1=d1[:, cut], op=ALU.mult)
            u_codes = mx.tile([P, PASSES * P], U32, align_bytes=64)
            u_scales = mx.tile([P, PASSES * P], U8, align_bytes=64)
            nc.vector.quantize_mx(out=u_codes[:].bitcast(FP8X4), scales=u_scales[:], in_=u_bf[:])
            u_of[i] = (u_codes, u_scales)

        def stage_c(i):
            u_codes, u_scales = u_of[i]
            out_sb = results.tile([P, D], F32)
            for n in range(D // N_OUT):
                cols = slice(n * N_OUT, (n + 1) * N_OUT)
                o_bank = psum_o.tile([P, BANK], F32)
                for g2 in range(PASSES):
                    nc.tensor.matmul_mx(
                        out=o_bank[:],
                        lhsT=u_codes[:, g2 * P : (g2 + 1) * P].bitcast(FP8X4),
                        lhsT_scale=u_scales[:, g2 * P : (g2 + 1) * P],
                        rhs=wi_codes[:, g2, cols].bitcast(FP8X4),
                        rhs_scale=wi_scales[:, g2, cols],
                        start=(g2 == 0),
                        stop=(g2 == PASSES - 1),
                    )
                nc.scalar.copy(out=out_sb[:, cols], in_=o_bank[:])
                nc.sync.dma_start(out=out_rows[i][:, cols], in_=out_sb[:, cols])

        stage_a(0)
        wj_codes, wj_scales = quantise_weight(wj_raw, "wj")
        stage_a(1)
        wi_codes, wi_scales = quantise_weight(wi_raw, "wi")
        for i in range(ROW_TILES):
            stage_b(i)
            if i + 2 < ROW_TILES:
                stage_a(i + 2)
            stage_c(i)
